import numpy as np
import ml_dtypes


def mxq(x, axis, fmt="e4m3"):
    dtype, down = {"e4m3": (ml_dtypes.float8_e4m3fn, 7), "e5m2": (ml_dtypes.float8_e5m2, 14)}[fmt]
    v = np.moveaxis(np.asarray(x, np.float32).astype(ml_dtypes.bfloat16).astype(np.float64), axis, -1)
    blocks = v.reshape(v.shape[:-1] + (-1, 32))
    amax = np.abs(blocks).max(-1, keepdims=True)
    byte = np.maximum(np.where(amax > 0, np.frexp(amax)[1] - 1 + 127, 0) - down, 1)
    scale = np.exp2(byte - 127.0)
    codes = (blocks / scale).astype(np.float32).astype(dtype).astype(np.float64)
    return np.moveaxis((codes * scale).reshape(v.shape), -1, axis)


WIDE = False


def mx_kscale(k):
    if not WIDE:
        return np.ones(k)
    levels = np.array([10, -10, 5, -5, 0])
    a = np.random.permutation(np.resize(levels, k // 512 * 4)).reshape(k // 512, 4)
    idx = np.arange(k)
    return np.exp2(a[idx // 512, idx % 128 // 32])


BF16 = ml_dtypes.bfloat16


def bf(x):
    return np.asarray(x, np.float32).astype(BF16)


def f64(x):
    return np.asarray(x).astype(np.float64)


E2M1 = np.array([0.0, 0.5, 1.0, 1.5, 2.0, 3.0, 4.0, 6.0, -0.0, -0.5, -1.0, -1.5, -2.0, -3.0, -4.0, -6.0])


def pack_weight(w, fmt):
    k, n = w.shape
    w = f64(bf(w)).reshape(k // 32, 32, n)
    amax = np.abs(w).max(1)
    if fmt == "e4m3":
        byte = np.frexp(amax)[1] - 1 + 127 - 7
    else:
        mant, ex = np.frexp(amax / 6.0)
        byte = np.where(mant > 0.5, ex, ex - 1) + 127
    byte = np.clip(np.where(amax > 0, byte, 1), 1, 254)
    scaled = (w * np.exp2(127.0 - byte)[:, None, :]).reshape(k, n).astype(np.float32)
    by_word = np.ascontiguousarray(scaled.reshape(k // 512, 128, 4, n).transpose(0, 1, 3, 2))
    if fmt == "e4m3":
        words = by_word.astype(ml_dtypes.float8_e4m3fn).view(np.uint8)
    else:
        c = by_word.astype(ml_dtypes.float4_e2m1fn).view(np.uint8) & 0xF
        words = c[..., 0::2] | (c[..., 1::2] << 4)
    return np.ascontiguousarray(words), np.ascontiguousarray(byte.astype(np.uint8).reshape(k // 512, 16, n))


def unpack_weight(words, scales, fmt):
    g, p, n, _ = words.shape
    if fmt == "e4m3":
        vals = np.ascontiguousarray(words).view(ml_dtypes.float8_e4m3fn).astype(np.float64)
    else:
        nib = np.empty((g, p, n, 4), np.uint8)
        nib[..., 0::2] = words & 0xF
        nib[..., 1::2] = words >> 4
        vals = E2M1[nib]
    vals = vals * np.repeat(np.exp2(scales.astype(np.float64) - 127.0), 8, axis=1)[..., None]
    return vals.transpose(0, 1, 3, 2).reshape(g * 512, n)

def pack4(w):
    words, scales = pack_weight(w, "e2m1")
    return words.reshape(words.shape[0], 128, -1), scales


def unpack4(words, scales):
    return unpack_weight(words.reshape(words.shape[0], 128, -1, 2), scales, "e2m1")


B, N, C = 8, 512, 512
R = B * N
G = 3 * C


def sigmoid(v):
    return 1.0 / (1.0 + np.exp(-v))


def setup_inputs():
    s = mx_kscale(C)
    s = s / s.max()
    x_proj = bf(np.random.standard_normal((R, G)))
    annotations = bf(np.random.standard_normal((B, N, C)) * s)
    words, scales = pack4(np.random.standard_normal((C, G)) / np.sqrt(C) / s[:, None])
    bias_h = bf(np.random.standard_normal(G) * 0.3)
    return {"x_proj": x_proj,
            "annotations": annotations,
            "recurrent_kernel_words": words,
            "recurrent_kernel_scales": scales,
            "bias_h": bias_h}


def reference(x_proj, annotations, recurrent_kernel_words, recurrent_kernel_scales, bias_h):
    b, n, c = annotations.shape
    h = f64(annotations).reshape(-1, c)
    mh = (mxq(h, 1, "e4m3") @ unpack4(recurrent_kernel_words, recurrent_kernel_scales)) + f64(bias_h)
    xz, xr, xh = np.split(f64(x_proj), 3, axis=-1)
    hz, hr, hh_in = np.split(mh, 3, axis=-1)
    z = sigmoid(xz + hz)
    r = sigmoid(xr + hr)
    hh = np.tanh(xh + r * hh_in)
    out = z * h + (1.0 - z) * hh
    return out.reshape(b, n, c)

@@ -1,0 +1,272 @@
+from contextlib import ExitStack
+
+import concourse.mybir as mybir
+from concourse.masks import make_identity
+
+F32 = mybir.dt.float32
+BF16 = mybir.dt.bfloat16
+I32 = mybir.dt.int32
+U8 = mybir.dt.uint8
+U32 = mybir.dt.uint32
+FP8X4 = mybir.dt.float8_e4m3fn_x4
+FP4X4 = mybir.dt.float4_e2m1fn_x4
+ALU = mybir.AluOpType
+ACT = mybir.ActivationFunctionType
+
+P = 128
+C = 512
+GATES = 3
+Z, R, CAND = 0, 1, 2
+NODES = 4096
+CHUNK = 512
+BLOCKS = CHUNK // P
+COL_TILES = C // P
+N_CHUNKS = NODES // CHUNK
+N_UNITS = N_CHUNKS * COL_TILES
+
+FLOPS = 2 * NODES * C * GATES * C
+
+
+def tile_gatedgraphconvolution_pb_t_kernel(
+    tc, x_proj, annotations, recurrent_kernel_words, recurrent_kernel_scales, bias_h, out
+):
+    nc = tc.nc
+    with ExitStack() as stack:
+        const = stack.enter_context(tc.tile_pool(name="const", bufs=1))
+        loads = stack.enter_context(tc.tile_pool(name="loads", bufs=3))
+        quant = stack.enter_context(tc.tile_pool(name="quant", bufs=2))
+        work2 = stack.enter_context(tc.tile_pool(name="work2", bufs=2))
+        work3 = stack.enter_context(tc.tile_pool(name="work3", bufs=3))
+        stores = stack.enter_context(tc.tile_pool(name="stores", bufs=2))
+        psum_mx = stack.enter_context(tc.psum_pool(name="psum_mx", bufs=3))
+        psum = stack.enter_context(tc.psum_pool(name="psum", bufs=1))
+        stack.enter_context(tc.manual_schedule())
+
+        chunk_tiles = {}
+        unit_tiles = {}
+
+        def load_h(c):
+            h_sb = loads.tile([P, BLOCKS, C], BF16, name="h_sb")
+            nc.sync.dma_start(out=h_sb[:], in_=annotations[c].rearrange("(p i) k -> p i k", i=BLOCKS))
+            chunk_tiles[("h_sb", c)] = h_sb
+
+        def load_x(c):
+            x_sb = loads.tile([P, BLOCKS, GATES * C], BF16, name="x_sb")
+            rows = x_proj[c * CHUNK : (c + 1) * CHUNK, :]
+            nc.sync.dma_start(out=x_sb[:], in_=rows.rearrange("(p i) g -> p i g", i=BLOCKS))
+            chunk_tiles[("x_sb", c)] = x_sb
+
+        def transpose_h_words(c, half):
+            h_sb = chunk_tiles[("h_sb", c)]
+            hw_ps = psum.tile([P, 2, 2, P], F32, name="hw_ps")
+            for b in range(2):
+                words = h_sb[:, 2 * half + b, :].bitcast(F32)
+                for u in range(2):
+                    nc.tensor.transpose(hw_ps[:, b, u, :], words[:, u : C // 2 : 2], ident_f32[:])
+            chunk_tiles[("hw_ps", c, half)] = hw_ps
+
+        def group_h_words(c, half):
+            if half == 0:
+                grouped_new = quant.tile([P, CHUNK * 4], BF16, name="grouped", align_bytes=64)
+                chunk_tiles[("grouped", c)] = grouped_new
+            grouped = chunk_tiles[("grouped", c)]
+            as_words = grouped[:].bitcast(F32).rearrange("p (i r u) -> p i r u", i=BLOCKS, u=2)
+            hw_ps = chunk_tiles[("hw_ps", c, half)]
+            nc.scalar.copy(
+                out=as_words[:, 2 * half : 2 * half + 2],
+                in_=hw_ps[:].rearrange("p b u r -> p b r u"),
+            )
+
+        def quantise_h(c):
+            codes = quant.tile([P, CHUNK], U32, name="codes", align_bytes=64)
+            scales = quant.tile([P, CHUNK], U8, name="scales", align_bytes=64)
+            nc.vector.quantize_mx(
+                out=codes[:].bitcast(FP8X4), scales=scales[:], in_=chunk_tiles[("grouped", c)][:]
+            )
+            chunk_tiles[("codes", c)] = codes
+            chunk_tiles[("scales", c)] = scales
+
+        def store_chunk(c):
+            nc.sync.dma_start(
+                out=out[c].rearrange("(p i) k -> p i k", i=BLOCKS), in_=chunk_tiles[("out_sb", c)][:]
+            )
+
+        def transpose_x(n, gates, name):
+            c, j = divmod(n, COL_TILES)
+            x_sb = chunk_tiles[("x_sb", c)]
+            xt_ps = psum.tile([P, len(gates), CHUNK], BF16, name=name)
+            for k, g in enumerate(gates):
+                first = g * C + j * P
+                for i in range(BLOCKS):
+                    nc.tensor.transpose(
+                        xt_ps[:, k, i * P : (i + 1) * P], x_sb[:, i, first : first + P], ident_bf16[:]
+                    )
+            unit_tiles[(name, n)] = xt_ps
+
+        def copy_xzr(n):
+            xzr_sb = work3.tile([P, 2, CHUNK], BF16, name="xzr_sb")
+            nc.scalar.copy(out=xzr_sb[:], in_=unit_tiles[("xzr_ps", n)][:])
+            unit_tiles[("xzr_sb", n)] = xzr_sb
+
+        def multiply(n):
+            c, j = divmod(n, COL_TILES)
+            for g, name in ((R, "hr_ps"), (Z, "hz_ps"), (CAND, "hc_ps")):
+                first = g * C + j * P
+                acc = psum_mx.tile([P, CHUNK], F32, name="acc")
+                nc.tensor.matmul_mx(
+                    out=acc[:],
+                    lhsT=w_words[:, 2 * first : 2 * (first + P)].bitcast(FP4X4),
+                    lhsT_scale=w_scales[:, first : first + P],
+                    rhs=chunk_tiles[("codes", c)][:].bitcast(FP8X4),
+                    rhs_scale=chunk_tiles[("scales", c)][:],
+                    start=True,
+                    stop=True,
+                )
+                unit_tiles[(name, n)] = acc
+
+        def bias_of(g, n):
+            column = g * COL_TILES + n % COL_TILES
+            return bias_sb[:, column : column + 1]
+
+        def add_x(n, k, acc_name, name):
+            pre = work2.tile([P, CHUNK], F32, name=name)
+            nc.vector.tensor_tensor(
+                out=pre[:], in0=unit_tiles[(acc_name, n)][:], in1=unit_tiles[("xzr_sb", n)][:, k, :], op=ALU.add
+            )
+            unit_tiles[(name, n)] = pre
+
+        def sigmoid(n, g, pre_name, pool, name):
+            gate = pool.tile([P, CHUNK], F32, name=name)
+            nc.scalar.activation(
+                out=gate[:], in_=unit_tiles[(pre_name, n)][:], func=ACT.Sigmoid, bias=bias_of(g, n), scale=1.0
+            )
+            unit_tiles[(name, n)] = gate
+
+        def reset(n):
+            rh = work2.tile([P, CHUNK], F32, name="rh")
+            nc.vector.scalar_tensor_tensor(
+                out=rh[:],
+                in0=unit_tiles[("hc_ps", n)][:],
+                scalar=bias_of(CAND, n),
+                in1=unit_tiles[("r", n)][:],
+                op0=ALU.add,
+                op1=ALU.mult,
+            )
+            unit_tiles[("rh", n)] = rh
+
+        def add_xh(n):
+            pre_c = work2.tile([P, CHUNK], F32, name="pre_c")
+            nc.vector.tensor_tensor(
+                out=pre_c[:], in0=unit_tiles[("rh", n)][:], in1=unit_tiles[("xh_ps", n)][:, 0, :], op=ALU.add
+            )
+            unit_tiles[("pre_c", n)] = pre_c
+
+        def tanh(n):
+            cand = work3.tile([P, CHUNK], F32, name="cand")
+            nc.scalar.activation(out=cand[:], in_=unit_tiles[("pre_c", n)][:], func=ACT.Tanh)
+            unit_tiles[("cand", n)] = cand
+
+        def transpose_h(n):
+            c, j = divmod(n, COL_TILES)
+            h_sb = chunk_tiles[("h_sb", c)]
+            ht_ps = psum.tile([P, CHUNK], BF16, name="ht_ps")
+            for i in range(BLOCKS):
+                nc.tensor.transpose(ht_ps[:, i * P : (i + 1) * P], h_sb[:, i, j * P : (j + 1) * P], ident_bf16[:])
+            unit_tiles[("ht_ps", n)] = ht_ps
+
+        def h_minus_cand(n):
+            diff = work2.tile([P, CHUNK], F32, name="diff")
+            nc.vector.tensor_tensor(
+                out=diff[:], in0=unit_tiles[("ht_ps", n)][:], in1=unit_tiles[("cand", n)][:], op=ALU.subtract
+            )
+            unit_tiles[("diff", n)] = diff
+
+        def mix(n):
+            zd = work2.tile([P, CHUNK], F32, name="zd")
+            nc.gpsimd.tensor_tensor(out=zd[:], in0=unit_tiles[("z", n)][:], in1=unit_tiles[("diff", n)][:], op=ALU.mult)
+            mixed = work3.tile([P, CHUNK], F32, name="mixed")
+            nc.gpsimd.tensor_tensor(out=mixed[:], in0=zd[:], in1=unit_tiles[("cand", n)][:], op=ALU.add)
+            unit_tiles[("mixed", n)] = mixed
+
+        def transpose_back(n):
+            mixed = unit_tiles[("mixed", n)]
+            ot_ps = psum.tile([P, BLOCKS, P], F32, name="ot_ps")
+            for i in range(BLOCKS):
+                nc.tensor.transpose(ot_ps[:, i, :], mixed[:, i * P : (i + 1) * P], ident_f32[:])
+            unit_tiles[("ot_ps", n)] = ot_ps
+
+        def copy_out(n):
+            c, j = divmod(n, COL_TILES)
+            if j == 0:
+                out_new = stores.tile([P, BLOCKS, C], F32, name="out_sb")
+                chunk_tiles[("out_sb", c)] = out_new
+            nc.scalar.copy(
+                out=chunk_tiles[("out_sb", c)][:, :, j * P : (j + 1) * P], in_=unit_tiles[("ot_ps", n)][:]
+            )
+
+        def for_unit(stage, n, *args):
+            if 0 <= n < N_UNITS:
+                stage(n, *args)
+
+        def for_chunk(stage, c, *args):
+            if 0 <= c < N_CHUNKS:
+                stage(c, *args)
+
+        bias_rows = const.tile([P, P], BF16, name="bias_rows")
+        nc.vector.memset(bias_rows[:], 0.0)
+        nc.sync.dma_start(out=bias_rows[0 : GATES * COL_TILES, :], in_=bias_h.rearrange("(r c) -> r c", c=P))
+        load_h(0)
+
+        w_scales = const.tile([P, GATES * C], U8, name="w_scales", align_bytes=64)
+        nc.vector.memset(w_scales[:].bitcast(I32), 0)
+        for quadrant in range(4):
+            nc.sync.dma_start(
+                out=w_scales[32 * quadrant : 32 * quadrant + 4, :].bitcast(I32),
+                in_=recurrent_kernel_scales[0, 4 * quadrant : 4 * quadrant + 4, :].bitcast(I32),
+            )
+        w_words = const.tile([P, 2 * GATES * C], U8, name="w_words", align_bytes=64)
+        nc.sync.dma_start(out=w_words[:].bitcast(I32), in_=recurrent_kernel_words[0].bitcast(I32))
+        load_x(0)
+
+        ident_bf16 = const.tile([P, P], BF16, name="ident_bf16")
+        make_identity(nc, ident_bf16[:])
+        ident_f32 = const.tile([P, P], F32, name="ident_f32")
+        make_identity(nc, ident_f32[:])
+
+        bias_ps = psum.tile([P, CHUNK], BF16, name="ht_ps")
+        nc.tensor.transpose(bias_ps[:, 0:P], bias_rows[:], ident_bf16[:])
+        bias_sb = const.tile([P, GATES * COL_TILES], F32, name="bias_sb")
+        nc.vector.tensor_copy(out=bias_sb[:], in_=bias_ps[:, 0 : GATES * COL_TILES])
+
+        for t in range(-5, N_UNITS + 3):
+            next_chunk, phase = divmod(t + 5, COL_TILES)
+
+            for_unit(reset, t)
+            for_unit(multiply, t + 1)
+            for_unit(sigmoid, t, Z, "pre_z", work3, "z")
+            for_unit(h_minus_cand, t - 1)
+            for_unit(copy_xzr, t + 2)
+            for_unit(mix, t - 1)
+            for_unit(transpose_h, t)
+            for_unit(transpose_x, t + 3, (Z, R), "xzr_ps")
+            for_unit(copy_out, t - 3)
+            if phase == 1:
+                for_chunk(load_h, next_chunk + 1)
+                for_chunk(load_x, next_chunk + 1)
+                for_chunk(group_h_words, next_chunk, 0)
+            if phase == 2:
+                for_chunk(group_h_words, next_chunk, 1)
+            if phase == 3:
+                for_chunk(quantise_h, next_chunk)
+                for_chunk(store_chunk, next_chunk - 2)
+            for_unit(add_x, t + 1, 1, "hr_ps", "pre_r")
+            for_unit(sigmoid, t + 1, R, "pre_r", work2, "r")
+            for_unit(transpose_back, t - 2)
+            if phase == 0:
+                for_chunk(transpose_h_words, next_chunk, 0)
+            if phase == 1:
+                for_chunk(transpose_h_words, next_chunk, 1)
+            for_unit(add_xh, t)
+            for_unit(tanh, t)
+            for_unit(add_x, t + 1, 0, "hz_ps", "pre_z")
+            for_unit(transpose_x, t + 1, (CAND,), "xh_ps")

@@ -33,37 +33,40 @@ def tile_gatedgraphconvolution_pb_t_kernel(
     nc = tc.nc
     with ExitStack() as stack:
         const = stack.enter_context(tc.tile_pool(name="const", bufs=1))
-        loads = stack.enter_context(tc.tile_pool(name="loads", bufs=3))
+        loads_x = stack.enter_context(tc.tile_pool(name="loads_x", bufs=5))
+        loads_h = stack.enter_context(tc.tile_pool(name="loads_h", bufs=6))
         quant = stack.enter_context(tc.tile_pool(name="quant", bufs=2))
         work2 = stack.enter_context(tc.tile_pool(name="work2", bufs=2))
         work3 = stack.enter_context(tc.tile_pool(name="work3", bufs=3))
-        stores = stack.enter_context(tc.tile_pool(name="stores", bufs=2))
-        psum_mx = stack.enter_context(tc.psum_pool(name="psum_mx", bufs=3))
+        work4 = stack.enter_context(tc.tile_pool(name="work4", bufs=4))
+        keep = stack.enter_context(tc.tile_pool(name="keep", bufs=10))
         psum = stack.enter_context(tc.psum_pool(name="psum", bufs=1))
+        psum2 = stack.enter_context(tc.psum_pool(name="psum2", bufs=2))
         stack.enter_context(tc.manual_schedule())
 
         chunk_tiles = {}
         unit_tiles = {}
 
         def load_h(c):
-            h_sb = loads.tile([P, BLOCKS, C], BF16, name="h_sb")
+            h_sb = loads_h.tile([P, BLOCKS, C], BF16, name="h_sb")
             nc.sync.dma_start(out=h_sb[:], in_=annotations[c].rearrange("(p i) k -> p i k", i=BLOCKS))
             chunk_tiles[("h_sb", c)] = h_sb
 
         def load_x(c):
-            x_sb = loads.tile([P, BLOCKS, GATES * C], BF16, name="x_sb")
+            x_sb = loads_x.tile([P, BLOCKS, GATES * C], BF16, name="x_sb")
             rows = x_proj[c * CHUNK : (c + 1) * CHUNK, :]
             nc.sync.dma_start(out=x_sb[:], in_=rows.rearrange("(p i) g -> p i g", i=BLOCKS))
             chunk_tiles[("x_sb", c)] = x_sb
 
-        def transpose_h_words(c, half):
-            h_sb = chunk_tiles[("h_sb", c)]
-            hw_ps = psum.tile([P, 2, 2, P], F32, name="hw_ps")
-            for b in range(2):
-                words = h_sb[:, 2 * half + b, :].bitcast(F32)
-                for u in range(2):
-                    nc.tensor.transpose(hw_ps[:, b, u, :], words[:, u : C // 2 : 2], ident_f32[:])
-            chunk_tiles[("hw_ps", c, half)] = hw_ps
+        def transpose_h_words(c, i):
+            half, b = divmod(i, 2)
+            if b == 0:
+                hw_new = psum.tile([P, 2, 2, P], F32, name="hw_ps")
+                chunk_tiles[("hw_ps", c, half)] = hw_new
+            hw_ps = chunk_tiles[("hw_ps", c, half)]
+            words = chunk_tiles[("h_sb", c)][:, i, :].bitcast(F32)
+            for u in range(2):
+                nc.tensor.transpose(hw_ps[:, b, u, :], words[:, u : C // 2 : 2], ident_f32[:])
 
         def group_h_words(c, half):
             if half == 0:
@@ -86,52 +89,46 @@ def tile_gatedgraphconvolution_pb_t_kernel(
             chunk_tiles[("codes", c)] = codes
             chunk_tiles[("scales", c)] = scales
 
-        def store_chunk(c):
-            nc.sync.dma_start(
-                out=out[c].rearrange("(p i) k -> p i k", i=BLOCKS), in_=chunk_tiles[("out_sb", c)][:]
-            )
-
-        def transpose_x(n, gates, name):
+        def transpose_x(n):
             c, j = divmod(n, COL_TILES)
             x_sb = chunk_tiles[("x_sb", c)]
-            xt_ps = psum.tile([P, len(gates), CHUNK], BF16, name=name)
-            for k, g in enumerate(gates):
+            xzr_ps = psum.tile([P, 2, CHUNK], BF16, name="xzr_ps")
+            for g in (Z, R):
                 first = g * C + j * P
                 for i in range(BLOCKS):
                     nc.tensor.transpose(
-                        xt_ps[:, k, i * P : (i + 1) * P], x_sb[:, i, first : first + P], ident_bf16[:]
+                        xzr_ps[:, g, i * P : (i + 1) * P], x_sb[:, i, first : first + P], ident_bf16[:]
                     )
-            unit_tiles[(name, n)] = xt_ps
+            unit_tiles[("xzr_ps", n)] = xzr_ps
 
         def copy_xzr(n):
             xzr_sb = work3.tile([P, 2, CHUNK], BF16, name="xzr_sb")
             nc.scalar.copy(out=xzr_sb[:], in_=unit_tiles[("xzr_ps", n)][:])
             unit_tiles[("xzr_sb", n)] = xzr_sb
 
-        def multiply(n):
+        def multiply(n, g, name):
             c, j = divmod(n, COL_TILES)
-            for g, name in ((R, "hr_ps"), (Z, "hz_ps"), (CAND, "hc_ps")):
-                first = g * C + j * P
-                acc = psum_mx.tile([P, CHUNK], F32, name="acc")
-                nc.tensor.matmul_mx(
-                    out=acc[:],
-                    lhsT=w_words[:, 2 * first : 2 * (first + P)].bitcast(FP4X4),
-                    lhsT_scale=w_scales[:, first : first + P],
-                    rhs=chunk_tiles[("codes", c)][:].bitcast(FP8X4),
-                    rhs_scale=chunk_tiles[("scales", c)][:],
-                    start=True,
-                    stop=True,
-                )
-                unit_tiles[(name, n)] = acc
+            first = g * C + j * P
+            acc = psum.tile([P, CHUNK], F32, name=name)
+            nc.tensor.matmul_mx(
+                out=acc[:],
+                lhsT=w_words[:, 2 * first : 2 * (first + P)].bitcast(FP4X4),
+                lhsT_scale=w_scales[:, first : first + P],
+                rhs=chunk_tiles[("codes", c)][:].bitcast(FP8X4),
+                rhs_scale=chunk_tiles[("scales", c)][:],
+                start=True,
+                stop=True,
+            )
+            unit_tiles[(name, n)] = acc
 
         def bias_of(g, n):
             column = g * COL_TILES + n % COL_TILES
             return bias_sb[:, column : column + 1]
 
-        def add_x(n, k, acc_name, name):
+        def add_x(n, g, acc_name, name):
             pre = work2.tile([P, CHUNK], F32, name=name)
             nc.vector.tensor_tensor(
-                out=pre[:], in0=unit_tiles[(acc_name, n)][:], in1=unit_tiles[("xzr_sb", n)][:, k, :], op=ALU.add
+                out=pre[:], in0=unit_tiles[(acc_name, n)][:], in1=unit_tiles[("xzr_sb", n)][:, g, :], op=ALU.add
             )
             unit_tiles[(name, n)] = pre
 
@@ -143,7 +140,7 @@ def tile_gatedgraphconvolution_pb_t_kernel(
             unit_tiles[(name, n)] = gate
 
         def reset(n):
-            rh = work2.tile([P, CHUNK], F32, name="rh")
+            rh = keep.tile([P, CHUNK], F32, name="rh")
             nc.vector.scalar_tensor_tensor(
                 out=rh[:],
                 in0=unit_tiles[("hc_ps", n)][:],
@@ -154,55 +151,65 @@ def tile_gatedgraphconvolution_pb_t_kernel(
             )
             unit_tiles[("rh", n)] = rh
 
-        def add_xh(n):
-            pre_c = work2.tile([P, CHUNK], F32, name="pre_c")
+        def candidate_input(m):
+            c, i = divmod(m, BLOCKS)
+            pc_ps = psum.tile([P, C], F32, name="pc_ps")
+            nc.tensor.matmul(
+                out=pc_ps[:],
+                lhsT=ident_bf16[:],
+                rhs=chunk_tiles[("x_sb", c)][:, i, CAND * C : (CAND + 1) * C],
+                start=True,
+                stop=False,
+            )
+            for j in range(COL_TILES):
+                nc.tensor.matmul(
+                    out=pc_ps[:, j * P : (j + 1) * P],
+                    lhsT=unit_tiles[("rh", c * COL_TILES + j)][:, i * P : (i + 1) * P],
+                    rhs=ident_f32[:],
+                    is_transpose=True,
+                    start=False,
+                    stop=(j == COL_TILES - 1),
+                )
+            unit_tiles[("pc_ps", m)] = pc_ps
+
+        def tanh(m):
+            cand = work4.tile([P, C], F32, name="cand")
+            nc.scalar.activation(out=cand[:], in_=unit_tiles[("pc_ps", m)][:], func=ACT.Tanh)
+            unit_tiles[("cand", m)] = cand
+
+        def transpose_z(m):
+            c, i = divmod(m, BLOCKS)
+            zb_ps = psum2.tile([P, C], F32, name="zb_ps")
+            for j in range(COL_TILES):
+                nc.tensor.transpose(
+                    zb_ps[:, j * P : (j + 1) * P],
+                    unit_tiles[("z", c * COL_TILES + j)][:, i * P : (i + 1) * P],
+                    ident_f32[:],
+                )
+            unit_tiles[("zb_ps", m)] = zb_ps
+
+        def h_minus_cand(m):
+            c, i = divmod(m, BLOCKS)
+            diff = work3.tile([P, C], F32, name="diff")
+            nc.gpsimd.tensor_tensor(
+                out=diff[:], in0=chunk_tiles[("h_sb", c)][:, i, :], in1=unit_tiles[("cand", m)][:], op=ALU.subtract
+            )
+            unit_tiles[("diff", m)] = diff
+
+        def times_z(m):
+            zd = work3.tile([P, C], F32, name="zd")
             nc.vector.tensor_tensor(
-                out=pre_c[:], in0=unit_tiles[("rh", n)][:], in1=unit_tiles[("xh_ps", n)][:, 0, :], op=ALU.add
+                out=zd[:], in0=unit_tiles[("zb_ps", m)][:], in1=unit_tiles[("diff", m)][:], op=ALU.mult
             )
-            unit_tiles[("pre_c", n)] = pre_c
+            unit_tiles[("zd", m)] = zd
 
-        def tanh(n):
-            cand = work3.tile([P, CHUNK], F32, name="cand")
-            nc.scalar.activation(out=cand[:], in_=unit_tiles[("pre_c", n)][:], func=ACT.Tanh)
-            unit_tiles[("cand", n)] = cand
-
-        def transpose_h(n):
-            c, j = divmod(n, COL_TILES)
-            h_sb = chunk_tiles[("h_sb", c)]
-            ht_ps = psum.tile([P, CHUNK], BF16, name="ht_ps")
-            for i in range(BLOCKS):
-                nc.tensor.transpose(ht_ps[:, i * P : (i + 1) * P], h_sb[:, i, j * P : (j + 1) * P], ident_bf16[:])
-            unit_tiles[("ht_ps", n)] = ht_ps
-
-        def h_minus_cand(n):
-            diff = work2.tile([P, CHUNK], F32, name="diff")
-            nc.vector.tensor_tensor(
-                out=diff[:], in0=unit_tiles[("ht_ps", n)][:], in1=unit_tiles[("cand", n)][:], op=ALU.subtract
+        def mix_and_store(m):
+            c, i = divmod(m, BLOCKS)
+            out_sb = work4.tile([P, C], F32, name="out_sb")
+            nc.gpsimd.tensor_tensor(
+                out=out_sb[:], in0=unit_tiles[("zd", m)][:], in1=unit_tiles[("cand", m)][:], op=ALU.add
             )
-            unit_tiles[("diff", n)] = diff
-
-        def mix(n):
-            zd = work2.tile([P, CHUNK], F32, name="zd")
-            nc.gpsimd.tensor_tensor(out=zd[:], in0=unit_tiles[("z", n)][:], in1=unit_tiles[("diff", n)][:], op=ALU.mult)
-            mixed = work3.tile([P, CHUNK], F32, name="mixed")
-            nc.gpsimd.tensor_tensor(out=mixed[:], in0=zd[:], in1=unit_tiles[("cand", n)][:], op=ALU.add)
-            unit_tiles[("mixed", n)] = mixed
-
-        def transpose_back(n):
-            mixed = unit_tiles[("mixed", n)]
-            ot_ps = psum.tile([P, BLOCKS, P], F32, name="ot_ps")
-            for i in range(BLOCKS):
-                nc.tensor.transpose(ot_ps[:, i, :], mixed[:, i * P : (i + 1) * P], ident_f32[:])
-            unit_tiles[("ot_ps", n)] = ot_ps
-
-        def copy_out(n):
-            c, j = divmod(n, COL_TILES)
-            if j == 0:
-                out_new = stores.tile([P, BLOCKS, C], F32, name="out_sb")
-                chunk_tiles[("out_sb", c)] = out_new
-            nc.scalar.copy(
-                out=chunk_tiles[("out_sb", c)][:, :, j * P : (j + 1) * P], in_=unit_tiles[("ot_ps", n)][:]
-            )
+            nc.sync.dma_start(out=out[c].rearrange("(p i) k -> p i k", i=BLOCKS)[:, i, :], in_=out_sb[:])
 
         def for_unit(stage, n, *args):
             if 0 <= n < N_UNITS:
@@ -233,40 +240,37 @@ def tile_gatedgraphconvolution_pb_t_kernel(
         ident_f32 = const.tile([P, P], F32, name="ident_f32")
         make_identity(nc, ident_f32[:])
 
-        bias_ps = psum.tile([P, CHUNK], BF16, name="ht_ps")
-        nc.tensor.transpose(bias_ps[:, 0:P], bias_rows[:], ident_bf16[:])
+        bias_ps = psum.tile([P, 2, CHUNK], BF16, name="xzr_ps")
+        nc.tensor.transpose(bias_ps[:, 0, 0:P], bias_rows[:], ident_bf16[:])
         bias_sb = const.tile([P, GATES * COL_TILES], F32, name="bias_sb")
-        nc.vector.tensor_copy(out=bias_sb[:], in_=bias_ps[:, 0 : GATES * COL_TILES])
+        nc.vector.tensor_copy(out=bias_sb[:], in_=bias_ps[:, 0, 0 : GATES * COL_TILES])
 
-        for t in range(-5, N_UNITS + 3):
-            next_chunk, phase = divmod(t + 5, COL_TILES)
+        for t in range(-7, N_UNITS + 6):
+            prep_chunk, block = divmod(t + 7, BLOCKS)
 
-            for_unit(reset, t)
-            for_unit(multiply, t + 1)
-            for_unit(sigmoid, t, Z, "pre_z", work3, "z")
-            for_unit(h_minus_cand, t - 1)
-            for_unit(copy_xzr, t + 2)
-            for_unit(mix, t - 1)
-            for_unit(transpose_h, t)
-            for_unit(transpose_x, t + 3, (Z, R), "xzr_ps")
-            for_unit(copy_out, t - 3)
-            if phase == 1:
-                for_chunk(load_h, next_chunk + 1)
-                for_chunk(load_x, next_chunk + 1)
-                for_chunk(group_h_words, next_chunk, 0)
-            if phase == 2:
-                for_chunk(group_h_words, next_chunk, 1)
-            if phase == 3:
-                for_chunk(quantise_h, next_chunk)
-                for_chunk(store_chunk, next_chunk - 2)
-            for_unit(add_x, t + 1, 1, "hr_ps", "pre_r")
+            for_unit(multiply, t + 1, R, "hr_ps")
+            for_unit(multiply, t + 1, Z, "hz_ps")
+            for_unit(h_minus_cand, t - 4)
+            for_unit(add_x, t + 1, R, "hr_ps", "pre_r")
+            if block == 2:
+                for_chunk(group_h_words, prep_chunk, 0)
+            if block == 0:
+                for_chunk(group_h_words, prep_chunk - 1, 1)
             for_unit(sigmoid, t + 1, R, "pre_r", work2, "r")
-            for_unit(transpose_back, t - 2)
-            if phase == 0:
-                for_chunk(transpose_h_words, next_chunk, 0)
-            if phase == 1:
-                for_chunk(transpose_h_words, next_chunk, 1)
-            for_unit(add_xh, t)
-            for_unit(tanh, t)
-            for_unit(add_x, t + 1, 0, "hz_ps", "pre_z")
-            for_unit(transpose_x, t + 1, (CAND,), "xh_ps")
+            for_unit(transpose_x, t + 2)
+            for_chunk(transpose_h_words, prep_chunk, block)
+            for_unit(add_x, t + 1, Z, "hz_ps", "pre_z")
+            for_unit(copy_xzr, t + 2)
+            for_unit(times_z, t - 5)
+            for_unit(mix_and_store, t - 6)
+            for_unit(multiply, t + 1, CAND, "hc_ps")
+            for_unit(sigmoid, t + 1, Z, "pre_z", keep, "z")
+            for_unit(reset, t + 1)
+            for_unit(candidate_input, t - 3)
+            for_unit(transpose_z, t - 4)
+            for_unit(tanh, t - 3)
+            if block == 0:
+                for_chunk(quantise_h, prep_chunk - 1)
+                for_chunk(load_h, prep_chunk + 1)
+            if block == 2:
+                for_chunk(load_x, prep_chunk + 1)

@@ -33,7 +33,8 @@ def tile_gatedgraphconvolution_pb_t_kernel(
     nc = tc.nc
     with ExitStack() as stack:
         const = stack.enter_context(tc.tile_pool(name="const", bufs=1))
-        loads_x = stack.enter_context(tc.tile_pool(name="loads_x", bufs=5))
+        loads_xzr = stack.enter_context(tc.tile_pool(name="loads_xzr", bufs=3))
+        loads_xh = stack.enter_context(tc.tile_pool(name="loads_xh", bufs=4))
         loads_h = stack.enter_context(tc.tile_pool(name="loads_h", bufs=6))
         quant = stack.enter_context(tc.tile_pool(name="quant", bufs=2))
         work2 = stack.enter_context(tc.tile_pool(name="work2", bufs=2))
@@ -52,31 +53,35 @@ def tile_gatedgraphconvolution_pb_t_kernel(
             nc.sync.dma_start(out=h_sb[:], in_=annotations[c].rearrange("(p i) k -> p i k", i=BLOCKS))
             chunk_tiles[("h_sb", c)] = h_sb
 
-        def load_x(c):
-            x_sb = loads_x.tile([P, BLOCKS, GATES * C], BF16, name="x_sb")
-            rows = x_proj[c * CHUNK : (c + 1) * CHUNK, :]
-            nc.sync.dma_start(out=x_sb[:], in_=rows.rearrange("(p i) g -> p i g", i=BLOCKS))
-            chunk_tiles[("x_sb", c)] = x_sb
+        def load_xzr(c):
+            xzr_in = loads_xzr.tile([P, BLOCKS, 2 * C], BF16, name="xzr_in")
+            rows = x_proj[c * CHUNK : (c + 1) * CHUNK, 0 : 2 * C]
+            nc.sync.dma_start(out=xzr_in[:], in_=rows.rearrange("(p i) g -> p i g", i=BLOCKS))
+            chunk_tiles[("xzr_in", c)] = xzr_in
 
-        def transpose_h_words(c, i):
-            half, b = divmod(i, 2)
-            if b == 0:
-                hw_new = psum.tile([P, 2, 2, P], F32, name="hw_ps")
-                chunk_tiles[("hw_ps", c, half)] = hw_new
-            hw_ps = chunk_tiles[("hw_ps", c, half)]
-            words = chunk_tiles[("h_sb", c)][:, i, :].bitcast(F32)
-            for u in range(2):
-                nc.tensor.transpose(hw_ps[:, b, u, :], words[:, u : C // 2 : 2], ident_f32[:])
+        def load_xh(c):
+            xh_in = loads_xh.tile([P, BLOCKS, C], BF16, name="xh_in")
+            rows = x_proj[c * CHUNK : (c + 1) * CHUNK, CAND * C : (CAND + 1) * C]
+            nc.sync.dma_start(out=xh_in[:], in_=rows.rearrange("(p i) g -> p i g", i=BLOCKS))
+            chunk_tiles[("xh_in", c)] = xh_in
 
-        def group_h_words(c, half):
-            if half == 0:
+        def transpose_h_words(c, blocks, name):
+            hw_ps = psum.tile([P, len(blocks), 2, P], F32, name=name)
+            for b, i in enumerate(blocks):
+                words = chunk_tiles[("h_sb", c)][:, i, :].bitcast(F32)
+                for u in range(2):
+                    nc.tensor.transpose(hw_ps[:, b, u, :], words[:, u : C // 2 : 2], ident_f32[:])
+            chunk_tiles[("hw_ps", c, blocks[0])] = hw_ps
+
+        def group_h_words(c, blocks, copy):
+            if blocks[0] == 0:
                 grouped_new = quant.tile([P, CHUNK * 4], BF16, name="grouped", align_bytes=64)
                 chunk_tiles[("grouped", c)] = grouped_new
             grouped = chunk_tiles[("grouped", c)]
             as_words = grouped[:].bitcast(F32).rearrange("p (i r u) -> p i r u", i=BLOCKS, u=2)
-            hw_ps = chunk_tiles[("hw_ps", c, half)]
-            nc.scalar.copy(
-                out=as_words[:, 2 * half : 2 * half + 2],
+            hw_ps = chunk_tiles[("hw_ps", c, blocks[0])]
+            copy(
+                out=as_words[:, blocks[0] : blocks[0] + len(blocks)],
                 in_=hw_ps[:].rearrange("p b u r -> p b r u"),
             )
 
@@ -91,7 +96,7 @@ def tile_gatedgraphconvolution_pb_t_kernel(
 
         def transpose_x(n):
             c, j = divmod(n, COL_TILES)
-            x_sb = chunk_tiles[("x_sb", c)]
+            x_sb = chunk_tiles[("xzr_in", c)]
             xzr_ps = psum.tile([P, 2, CHUNK], BF16, name="xzr_ps")
             for g in (Z, R):
                 first = g * C + j * P
@@ -153,11 +158,12 @@ def tile_gatedgraphconvolution_pb_t_kernel(
 
         def candidate_input(m):
             c, i = divmod(m, BLOCKS)
-            pc_ps = psum.tile([P, C], F32, name="pc_ps")
+            last = c == N_CHUNKS - 1
+            pc_ps = psum.tile([P, C], F32, name=("pc_ps", "hr_ps", "hz_ps", "hc_ps")[i] if last else "pc_ps")
             nc.tensor.matmul(
                 out=pc_ps[:],
                 lhsT=ident_bf16[:],
-                rhs=chunk_tiles[("x_sb", c)][:, i, CAND * C : (CAND + 1) * C],
+                rhs=chunk_tiles[("xh_in", c)][:, i, :],
                 start=True,
                 stop=False,
             )
@@ -188,10 +194,10 @@ def tile_gatedgraphconvolution_pb_t_kernel(
                 )
             unit_tiles[("zb_ps", m)] = zb_ps
 
-        def h_minus_cand(m):
+        def h_minus_cand(m, eng):
             c, i = divmod(m, BLOCKS)
             diff = work3.tile([P, C], F32, name="diff")
-            nc.gpsimd.tensor_tensor(
+            eng.tensor_tensor(
                 out=diff[:], in0=chunk_tiles[("h_sb", c)][:, i, :], in1=unit_tiles[("cand", m)][:], op=ALU.subtract
             )
             unit_tiles[("diff", m)] = diff
@@ -203,10 +209,10 @@ def tile_gatedgraphconvolution_pb_t_kernel(
             )
             unit_tiles[("zd", m)] = zd
 
-        def mix_and_store(m):
+        def add_and_store(m, eng):
             c, i = divmod(m, BLOCKS)
             out_sb = work4.tile([P, C], F32, name="out_sb")
-            nc.gpsimd.tensor_tensor(
+            eng.tensor_tensor(
                 out=out_sb[:], in0=unit_tiles[("zd", m)][:], in1=unit_tiles[("cand", m)][:], op=ALU.add
             )
             nc.sync.dma_start(out=out[c].rearrange("(p i) k -> p i k", i=BLOCKS)[:, i, :], in_=out_sb[:])
@@ -233,7 +239,12 @@ def tile_gatedgraphconvolution_pb_t_kernel(
             )
         w_words = const.tile([P, 2 * GATES * C], U8, name="w_words", align_bytes=64)
         nc.sync.dma_start(out=w_words[:].bitcast(I32), in_=recurrent_kernel_words[0].bitcast(I32))
-        load_x(0)
+        load_xzr(0)
+        load_h(1)
+        load_xh(0)
+        load_xzr(1)
+        load_h(2)
+        load_xh(1)
 
         ident_bf16 = const.tile([P, P], BF16, name="ident_bf16")
         make_identity(nc, ident_bf16[:])
@@ -245,32 +256,45 @@ def tile_gatedgraphconvolution_pb_t_kernel(
         bias_sb = const.tile([P, GATES * COL_TILES], F32, name="bias_sb")
         nc.vector.tensor_copy(out=bias_sb[:], in_=bias_ps[:, 0, 0 : GATES * COL_TILES])
 
-        for t in range(-7, N_UNITS + 6):
-            prep_chunk, block = divmod(t + 7, BLOCKS)
+        transpose_h_words(0, (0, 1), "hw_ps")
+        transpose_h_words(0, (2, 3), "pc_ps")
+        group_h_words(0, (0, 1), nc.scalar.copy)
+        group_h_words(0, (2, 3), nc.vector.tensor_copy)
+        quantise_h(0)
 
-            for_unit(multiply, t + 1, R, "hr_ps")
-            for_unit(multiply, t + 1, Z, "hz_ps")
-            for_unit(h_minus_cand, t - 4)
-            for_unit(add_x, t + 1, R, "hr_ps", "pre_r")
-            if block == 2:
-                for_chunk(group_h_words, prep_chunk, 0)
-            if block == 0:
-                for_chunk(group_h_words, prep_chunk - 1, 1)
-            for_unit(sigmoid, t + 1, R, "pre_r", work2, "r")
+        def engine_for(m, first):
+            return nc.vector if m >= first else nc.gpsimd
+
+        for t in range(-2, N_UNITS + 8):
+            prep_chunk, block = divmod(t + 6, BLOCKS)
+            late_chunk, late_block = divmod(t + 5, BLOCKS)
+            this_chunk, phase = divmod(t, BLOCKS)
+
+            for_unit(copy_xzr, t + 1)
+            if late_chunk >= 1:
+                for_chunk(group_h_words, late_chunk, (late_block,), nc.scalar.copy)
+            for_unit(multiply, t, R, "hr_ps")
+            for_unit(multiply, t, Z, "hz_ps")
+            for_unit(multiply, t - 1, CAND, "hc_ps")
+            for_unit(candidate_input, t - 5)
+            for_unit(transpose_z, t - 6)
             for_unit(transpose_x, t + 2)
-            for_chunk(transpose_h_words, prep_chunk, block)
-            for_unit(add_x, t + 1, Z, "hz_ps", "pre_z")
-            for_unit(copy_xzr, t + 2)
-            for_unit(times_z, t - 5)
-            for_unit(mix_and_store, t - 6)
-            for_unit(multiply, t + 1, CAND, "hc_ps")
-            for_unit(sigmoid, t + 1, Z, "pre_z", keep, "z")
-            for_unit(reset, t + 1)
-            for_unit(candidate_input, t - 3)
-            for_unit(transpose_z, t - 4)
-            for_unit(tanh, t - 3)
-            if block == 0:
-                for_chunk(quantise_h, prep_chunk - 1)
-                for_chunk(load_h, prep_chunk + 1)
-            if block == 2:
-                for_chunk(load_x, prep_chunk + 1)
+            if prep_chunk >= 1:
+                for_chunk(transpose_h_words, prep_chunk, (block,), "hw_ps")
+            for_unit(h_minus_cand, t - 6, engine_for(t - 6, 32))
+            for_unit(add_x, t, R, "hr_ps", "pre_r")
+            for_unit(sigmoid, t, R, "pre_r", work3, "r")
+            for_unit(tanh, t - 5)
+            for_unit(add_x, t, Z, "hz_ps", "pre_z")
+            for_unit(sigmoid, t, Z, "pre_z", keep, "z")
+            for_unit(reset, t - 1)
+            for_unit(times_z, t - 6)
+            for_unit(add_and_store, t - 7, engine_for(t - 7, 24))
+            if late_block == 3 and late_chunk >= 1:
+                for_chunk(quantise_h, late_chunk)
+            if this_chunk >= 0 and phase == 0:
+                for_chunk(load_h, this_chunk + 3)
+            if this_chunk >= 0 and phase == 1:
+                for_chunk(load_xzr, this_chunk + 2)
+            if this_chunk >= 0 and phase == 2:
+                for_chunk(load_xh, this_chunk + 2)

@@ -40,6 +40,7 @@ def tile_gatedgraphconvolution_pb_t_kernel(
         work2 = stack.enter_context(tc.tile_pool(name="work2", bufs=2))
         work3 = stack.enter_context(tc.tile_pool(name="work3", bufs=3))
         work4 = stack.enter_context(tc.tile_pool(name="work4", bufs=4))
+        work6 = stack.enter_context(tc.tile_pool(name="work6", bufs=6))
         keep = stack.enter_context(tc.tile_pool(name="keep", bufs=10))
         psum = stack.enter_context(tc.psum_pool(name="psum", bufs=1))
         psum2 = stack.enter_context(tc.psum_pool(name="psum2", bufs=2))
@@ -97,7 +98,10 @@ def tile_gatedgraphconvolution_pb_t_kernel(
         def transpose_x(n):
             c, j = divmod(n, COL_TILES)
             x_sb = chunk_tiles[("xzr_in", c)]
-            xzr_ps = psum.tile([P, 2, CHUNK], BF16, name="xzr_ps")
+            if n == 1:
+                xzr_ps = psum2.tile([P, 2, CHUNK], BF16, name="zb_ps")
+            else:
+                xzr_ps = psum.tile([P, 2, CHUNK], BF16, name="xzr_ps")
             for g in (Z, R):
                 first = g * C + j * P
                 for i in range(BLOCKS):
@@ -179,7 +183,7 @@ def tile_gatedgraphconvolution_pb_t_kernel(
             unit_tiles[("pc_ps", m)] = pc_ps
 
         def tanh(m):
-            cand = work4.tile([P, C], F32, name="cand")
+            cand = work6.tile([P, C], F32, name="cand")
             nc.scalar.activation(out=cand[:], in_=unit_tiles[("pc_ps", m)][:], func=ACT.Tanh)
             unit_tiles[("cand", m)] = cand
 
@@ -265,14 +269,10 @@ def tile_gatedgraphconvolution_pb_t_kernel(
         def engine_for(m, first):
             return nc.vector if m >= first else nc.gpsimd
 
-        for t in range(-2, N_UNITS + 8):
+        for t in range(-3, N_UNITS + 9):
             prep_chunk, block = divmod(t + 6, BLOCKS)
-            late_chunk, late_block = divmod(t + 5, BLOCKS)
             this_chunk, phase = divmod(t, BLOCKS)
 
-            for_unit(copy_xzr, t + 1)
-            if late_chunk >= 1:
-                for_chunk(group_h_words, late_chunk, (late_block,), nc.scalar.copy)
             for_unit(multiply, t, R, "hr_ps")
             for_unit(multiply, t, Z, "hz_ps")
             for_unit(multiply, t - 1, CAND, "hc_ps")
@@ -281,17 +281,20 @@ def tile_gatedgraphconvolution_pb_t_kernel(
             for_unit(transpose_x, t + 2)
             if prep_chunk >= 1:
                 for_chunk(transpose_h_words, prep_chunk, (block,), "hw_ps")
-            for_unit(h_minus_cand, t - 6, engine_for(t - 6, 32))
+            for_unit(h_minus_cand, t - 6, nc.gpsimd)
             for_unit(add_x, t, R, "hr_ps", "pre_r")
-            for_unit(sigmoid, t, R, "pre_r", work3, "r")
             for_unit(tanh, t - 5)
+            for_unit(sigmoid, t, R, "pre_r", work3, "r")
+            for_unit(copy_xzr, t + 2)
+            if divmod(t + 6, BLOCKS)[0] >= 1:
+                for_chunk(group_h_words, divmod(t + 6, BLOCKS)[0], (divmod(t + 6, BLOCKS)[1],), nc.scalar.copy)
             for_unit(add_x, t, Z, "hz_ps", "pre_z")
             for_unit(sigmoid, t, Z, "pre_z", keep, "z")
             for_unit(reset, t - 1)
             for_unit(times_z, t - 6)
             for_unit(add_and_store, t - 7, engine_for(t - 7, 24))
-            if late_block == 3 and late_chunk >= 1:
-                for_chunk(quantise_h, late_chunk)
+            if divmod(t + 5, BLOCKS)[1] == 3 and divmod(t + 5, BLOCKS)[0] >= 1:
+                for_chunk(quantise_h, divmod(t + 5, BLOCKS)[0])
             if this_chunk >= 0 and phase == 0:
                 for_chunk(load_h, this_chunk + 3)
             if this_chunk >= 0 and phase == 1:

@@ -279,15 +279,19 @@ def tile_gatedgraphconvolution_pb_t_kernel(
             for_unit(candidate_input, t - 5)
             for_unit(transpose_z, t - 6)
             for_unit(transpose_x, t + 2)
-            if prep_chunk >= 1:
+            if prep_chunk >= 2:
                 for_chunk(transpose_h_words, prep_chunk, (block,), "hw_ps")
+            if t in (0, 1):
+                transpose_h_words(1, (2 * t, 2 * t + 1), "hw_ps")
             for_unit(h_minus_cand, t - 6, nc.gpsimd)
             for_unit(add_x, t, R, "hr_ps", "pre_r")
             for_unit(tanh, t - 5)
             for_unit(sigmoid, t, R, "pre_r", work3, "r")
             for_unit(copy_xzr, t + 2)
-            if divmod(t + 6, BLOCKS)[0] >= 1:
-                for_chunk(group_h_words, divmod(t + 6, BLOCKS)[0], (divmod(t + 6, BLOCKS)[1],), nc.scalar.copy)
+            if prep_chunk >= 2:
+                for_chunk(group_h_words, prep_chunk, (block,), nc.scalar.copy)
+            if t in (0, 1):
+                group_h_words(1, (2 * t, 2 * t + 1), nc.scalar.copy)
             for_unit(add_x, t, Z, "hz_ps", "pre_z")
             for_unit(sigmoid, t, Z, "pre_z", keep, "z")
             for_unit(reset, t - 1)

@@ -99,7 +99,7 @@ def tile_gatedgraphconvolution_pb_t_kernel(
             c, j = divmod(n, COL_TILES)
             x_sb = chunk_tiles[("xzr_in", c)]
             if n == 1:
-                xzr_ps = psum2.tile([P, 2, CHUNK], BF16, name="zb_ps")
+                xzr_ps = psum.tile([P, 2, CHUNK], BF16, name="zb_ps")
             else:
                 xzr_ps = psum.tile([P, 2, CHUNK], BF16, name="xzr_ps")
             for g in (Z, R):
@@ -118,7 +118,7 @@ def tile_gatedgraphconvolution_pb_t_kernel(
         def multiply(n, g, name):
             c, j = divmod(n, COL_TILES)
             first = g * C + j * P
-            acc = psum.tile([P, CHUNK], F32, name=name)
+            acc = (psum2 if g == CAND else psum).tile([P, CHUNK], F32, name=name)
             nc.tensor.matmul_mx(
                 out=acc[:],
                 lhsT=w_words[:, 2 * first : 2 * (first + P)].bitcast(FP4X4),
@@ -163,7 +163,7 @@ def tile_gatedgraphconvolution_pb_t_kernel(
         def candidate_input(m):
             c, i = divmod(m, BLOCKS)
             last = c == N_CHUNKS - 1
-            pc_ps = psum.tile([P, C], F32, name=("pc_ps", "hr_ps", "hz_ps", "hc_ps")[i] if last else "pc_ps")
+            pc_ps = psum.tile([P, C], F32, name=("pc_ps", "hr_ps", "hz_ps", "xzr_ps")[i] if last else "pc_ps")
             nc.tensor.matmul(
                 out=pc_ps[:],
                 lhsT=ident_bf16[:],
@@ -189,7 +189,10 @@ def tile_gatedgraphconvolution_pb_t_kernel(
 
         def transpose_z(m):
             c, i = divmod(m, BLOCKS)
-            zb_ps = psum2.tile([P, C], F32, name="zb_ps")
+            if c == N_CHUNKS - 1 and i >= 2:
+                zb_ps = psum2.tile([P, C], F32, name="hc_ps")
+            else:
+                zb_ps = psum.tile([P, C], F32, name="hw_ps" if c == N_CHUNKS - 1 and i == 1 else "zb_ps")
             for j in range(COL_TILES):
                 nc.tensor.transpose(
                     zb_ps[:, j * P : (j + 1) * P],

@@ -39,7 +39,7 @@ def tile_gatedgraphconvolution_pb_t_kernel(
         quant = stack.enter_context(tc.tile_pool(name="quant", bufs=2))
         work2 = stack.enter_context(tc.tile_pool(name="work2", bufs=2))
         work3 = stack.enter_context(tc.tile_pool(name="work3", bufs=3))
-        work4 = stack.enter_context(tc.tile_pool(name="work4", bufs=4))
+        outs = stack.enter_context(tc.tile_pool(name="outs", bufs=3))
         work6 = stack.enter_context(tc.tile_pool(name="work6", bufs=6))
         keep = stack.enter_context(tc.tile_pool(name="keep", bufs=10))
         psum = stack.enter_context(tc.psum_pool(name="psum", bufs=1))
@@ -160,69 +160,76 @@ def tile_gatedgraphconvolution_pb_t_kernel(
             )
             unit_tiles[("rh", n)] = rh
 
-        def candidate_input(m):
-            c, i = divmod(m, BLOCKS)
-            last = c == N_CHUNKS - 1
-            pc_ps = psum.tile([P, C], F32, name=("pc_ps", "hr_ps", "hz_ps", "xzr_ps")[i] if last else "pc_ps")
+        def cols_of(n):
+            j = n % COL_TILES
+            return slice(j * P, (j + 1) * P)
+
+        def candidate_input(n):
+            c = n // COL_TILES
+            pc_ps = psum.tile([P, BLOCKS, P], F32, name="pc_ps")
             nc.tensor.matmul(
                 out=pc_ps[:],
                 lhsT=ident_bf16[:],
-                rhs=chunk_tiles[("xh_in", c)][:, i, :],
+                rhs=chunk_tiles[("xh_in", c)][:, :, cols_of(n)],
                 start=True,
                 stop=False,
             )
-            for j in range(COL_TILES):
+            for i in range(BLOCKS):
                 nc.tensor.matmul(
-                    out=pc_ps[:, j * P : (j + 1) * P],
-                    lhsT=unit_tiles[("rh", c * COL_TILES + j)][:, i * P : (i + 1) * P],
+                    out=pc_ps[:, i, :],
+                    lhsT=unit_tiles[("rh", n)][:, i * P : (i + 1) * P],
                     rhs=ident_f32[:],
                     is_transpose=True,
                     start=False,
-                    stop=(j == COL_TILES - 1),
+                    stop=(i == BLOCKS - 1),
                 )
-            unit_tiles[("pc_ps", m)] = pc_ps
+            unit_tiles[("pc_ps", n)] = pc_ps
 
-        def tanh(m):
-            cand = work6.tile([P, C], F32, name="cand")
-            nc.scalar.activation(out=cand[:], in_=unit_tiles[("pc_ps", m)][:], func=ACT.Tanh)
-            unit_tiles[("cand", m)] = cand
+        def tanh(n):
+            cand = work6.tile([P, BLOCKS, P], F32, name="cand")
+            nc.scalar.activation(out=cand[:], in_=unit_tiles[("pc_ps", n)][:], func=ACT.Tanh)
+            unit_tiles[("cand", n)] = cand
 
-        def transpose_z(m):
-            c, i = divmod(m, BLOCKS)
-            if c == N_CHUNKS - 1 and i >= 2:
-                zb_ps = psum2.tile([P, C], F32, name="hc_ps")
-            else:
-                zb_ps = psum.tile([P, C], F32, name="hw_ps" if c == N_CHUNKS - 1 and i == 1 else "zb_ps")
-            for j in range(COL_TILES):
+        def transpose_z(n):
+            zb_ps = psum.tile([P, BLOCKS, P], F32, name="zb_ps")
+            for i in range(BLOCKS):
                 nc.tensor.transpose(
-                    zb_ps[:, j * P : (j + 1) * P],
-                    unit_tiles[("z", c * COL_TILES + j)][:, i * P : (i + 1) * P],
-                    ident_f32[:],
+                    zb_ps[:, i, :], unit_tiles[("z", n)][:, i * P : (i + 1) * P], ident_f32[:]
                 )
-            unit_tiles[("zb_ps", m)] = zb_ps
+            unit_tiles[("zb_ps", n)] = zb_ps
 
-        def h_minus_cand(m, eng):
-            c, i = divmod(m, BLOCKS)
-            diff = work3.tile([P, C], F32, name="diff")
+        def h_minus_cand(n, eng):
+            c = n // COL_TILES
+            diff = work3.tile([P, BLOCKS, P], F32, name="diff")
             eng.tensor_tensor(
-                out=diff[:], in0=chunk_tiles[("h_sb", c)][:, i, :], in1=unit_tiles[("cand", m)][:], op=ALU.subtract
+                out=diff[:],
+                in0=chunk_tiles[("h_sb", c)][:, :, cols_of(n)],
+                in1=unit_tiles[("cand", n)][:],
+                op=ALU.subtract,
             )
-            unit_tiles[("diff", m)] = diff
+            unit_tiles[("diff", n)] = diff
 
-        def times_z(m):
-            zd = work3.tile([P, C], F32, name="zd")
+        def times_z(n):
+            zd = work3.tile([P, BLOCKS, P], F32, name="zd")
             nc.vector.tensor_tensor(
-                out=zd[:], in0=unit_tiles[("zb_ps", m)][:], in1=unit_tiles[("diff", m)][:], op=ALU.mult
+                out=zd[:], in0=unit_tiles[("zb_ps", n)][:], in1=unit_tiles[("diff", n)][:], op=ALU.mult
             )
-            unit_tiles[("zd", m)] = zd
+            unit_tiles[("zd", n)] = zd
 
-        def add_and_store(m, eng):
-            c, i = divmod(m, BLOCKS)
-            out_sb = work4.tile([P, C], F32, name="out_sb")
+        def add_and_store(n, eng):
+            c, j = divmod(n, COL_TILES)
+            if j == 0:
+                out_new = outs.tile([P, BLOCKS, C], F32, name="out_sb")
+                chunk_tiles[("out_sb", c)] = out_new
+            out_sb = chunk_tiles[("out_sb", c)]
             eng.tensor_tensor(
-                out=out_sb[:], in0=unit_tiles[("zd", m)][:], in1=unit_tiles[("cand", m)][:], op=ALU.add
+                out=out_sb[:, :, cols_of(n)], in0=unit_tiles[("zd", n)][:], in1=unit_tiles[("cand", n)][:], op=ALU.add
             )
-            nc.sync.dma_start(out=out[c].rearrange("(p i) k -> p i k", i=BLOCKS)[:, i, :], in_=out_sb[:])
+            rows = out[c].rearrange("(p i) k -> p i k", i=BLOCKS)
+            if c == N_CHUNKS - 1:
+                nc.sync.dma_start(out=rows[:, :, cols_of(n)], in_=out_sb[:, :, cols_of(n)])
+            elif j == COL_TILES - 1:
+                nc.sync.dma_start(out=rows, in_=out_sb[:])
 
         def for_unit(stage, n, *args):
             if 0 <= n < N_UNITS:
@@ -272,23 +279,23 @@ def tile_gatedgraphconvolution_pb_t_kernel(
         def engine_for(m, first):
             return nc.vector if m >= first else nc.gpsimd
 
-        for t in range(-3, N_UNITS + 9):
+        for t in range(-3, N_UNITS + 5):
             prep_chunk, block = divmod(t + 6, BLOCKS)
             this_chunk, phase = divmod(t, BLOCKS)
 
             for_unit(multiply, t, R, "hr_ps")
             for_unit(multiply, t, Z, "hz_ps")
             for_unit(multiply, t - 1, CAND, "hc_ps")
-            for_unit(candidate_input, t - 5)
-            for_unit(transpose_z, t - 6)
+            for_unit(candidate_input, t - 2)
+            for_unit(transpose_z, t - 3)
             for_unit(transpose_x, t + 2)
             if prep_chunk >= 2:
                 for_chunk(transpose_h_words, prep_chunk, (block,), "hw_ps")
             if t in (0, 1):
                 transpose_h_words(1, (2 * t, 2 * t + 1), "hw_ps")
-            for_unit(h_minus_cand, t - 6, nc.gpsimd)
+            for_unit(h_minus_cand, t - 3, nc.gpsimd)
             for_unit(add_x, t, R, "hr_ps", "pre_r")
-            for_unit(tanh, t - 5)
+            for_unit(tanh, t - 2)
             for_unit(sigmoid, t, R, "pre_r", work3, "r")
             for_unit(copy_xzr, t + 2)
             if prep_chunk >= 2:
@@ -298,8 +305,8 @@ def tile_gatedgraphconvolution_pb_t_kernel(
             for_unit(add_x, t, Z, "hz_ps", "pre_z")
             for_unit(sigmoid, t, Z, "pre_z", keep, "z")
             for_unit(reset, t - 1)
-            for_unit(times_z, t - 6)
-            for_unit(add_and_store, t - 7, engine_for(t - 7, 24))
+            for_unit(times_z, t - 3)
+            for_unit(add_and_store, t - 4, engine_for(t - 4, 28))
             if divmod(t + 5, BLOCKS)[1] == 3 and divmod(t + 5, BLOCKS)[0] >= 1:
                 for_chunk(quantise_h, divmod(t + 5, BLOCKS)[0])
             if this_chunk >= 0 and phase == 0:

@@ -60,6 +60,19 @@ def tile_gatedgraphconvolution_pb_t_kernel(
             nc.sync.dma_start(out=xzr_in[:], in_=rows.rearrange("(p i) g -> p i g", i=BLOCKS))
             chunk_tiles[("xzr_in", c)] = xzr_in
 
+        def load_x_first(g, half):
+            part = const.tile([P, BLOCKS, 2 * P], BF16, name="x_first_%d_%d" % (g, half))
+            first = g * C + half * 2 * P
+            rows = x_proj[0:CHUNK, first : first + 2 * P]
+            nc.sync.dma_start(out=part[:], in_=rows.rearrange("(p i) g -> p i g", i=BLOCKS))
+            chunk_tiles[("x_first", g, half)] = part
+
+        def x_block(c, g, j, i):
+            if c == 0:
+                return chunk_tiles[("x_first", g, j // 2)][:, i, (j % 2) * P : (j % 2 + 1) * P]
+            first = g * C + j * P
+            return chunk_tiles[("xzr_in", c)][:, i, first : first + P]
+
         def load_xh(c):
             xh_in = loads_xh.tile([P, BLOCKS, C], BF16, name="xh_in")
             rows = x_proj[c * CHUNK : (c + 1) * CHUNK, CAND * C : (CAND + 1) * C]
@@ -97,17 +110,13 @@ def tile_gatedgraphconvolution_pb_t_kernel(
 
         def transpose_x(n):
             c, j = divmod(n, COL_TILES)
-            x_sb = chunk_tiles[("xzr_in", c)]
             if n == 1:
                 xzr_ps = psum.tile([P, 2, CHUNK], BF16, name="zb_ps")
             else:
                 xzr_ps = psum.tile([P, 2, CHUNK], BF16, name="xzr_ps")
             for g in (Z, R):
-                first = g * C + j * P
                 for i in range(BLOCKS):
-                    nc.tensor.transpose(
-                        xzr_ps[:, g, i * P : (i + 1) * P], x_sb[:, i, first : first + P], ident_bf16[:]
-                    )
+                    nc.tensor.transpose(xzr_ps[:, g, i * P : (i + 1) * P], x_block(c, g, j, i), ident_bf16[:])
             unit_tiles[("xzr_ps", n)] = xzr_ps
 
         def copy_xzr(n):
@@ -166,7 +175,7 @@ def tile_gatedgraphconvolution_pb_t_kernel(
 
         def candidate_input(n):
             c = n // COL_TILES
-            pc_ps = psum.tile([P, BLOCKS, P], F32, name="pc_ps")
+            pc_ps = psum.tile([P, BLOCKS, P], F32, name={N_UNITS - 2: "hz_ps", N_UNITS - 1: "hr_ps"}.get(n, "pc_ps"))
             nc.tensor.matmul(
                 out=pc_ps[:],
                 lhsT=ident_bf16[:],
@@ -191,7 +200,7 @@ def tile_gatedgraphconvolution_pb_t_kernel(
             unit_tiles[("cand", n)] = cand
 
         def transpose_z(n):
-            zb_ps = psum.tile([P, BLOCKS, P], F32, name="zb_ps")
+            zb_ps = psum.tile([P, BLOCKS, P], F32, name={N_UNITS - 2: "xzr_ps", N_UNITS - 1: "hw_ps"}.get(n, "zb_ps"))
             for i in range(BLOCKS):
                 nc.tensor.transpose(
                     zb_ps[:, i, :], unit_tiles[("z", n)][:, i * P : (i + 1) * P], ident_f32[:]
@@ -239,10 +248,16 @@ def tile_gatedgraphconvolution_pb_t_kernel(
             if 0 <= c < N_CHUNKS:
                 stage(c, *args)
 
+        load_h(0)
+        warm_in = const.tile([P, 1], F32, name="warm_in")
+        nc.vector.memset(warm_in[:], 0.0)
+        warm_out = const.tile([P, 1], F32, name="warm_out")
+        nc.scalar.activation(out=warm_out[:], in_=warm_in[:], func=ACT.Sigmoid)
         bias_rows = const.tile([P, P], BF16, name="bias_rows")
         nc.vector.memset(bias_rows[:], 0.0)
         nc.sync.dma_start(out=bias_rows[0 : GATES * COL_TILES, :], in_=bias_h.rearrange("(r c) -> r c", c=P))
-        load_h(0)
+        load_x_first(R, 0)
+        load_x_first(Z, 0)
 
         w_scales = const.tile([P, GATES * C], U8, name="w_scales", align_bytes=64)
         nc.vector.memset(w_scales[:].bitcast(I32), 0)
@@ -253,7 +268,8 @@ def tile_gatedgraphconvolution_pb_t_kernel(
             )
         w_words = const.tile([P, 2 * GATES * C], U8, name="w_words", align_bytes=64)
         nc.sync.dma_start(out=w_words[:].bitcast(I32), in_=recurrent_kernel_words[0].bitcast(I32))
-        load_xzr(0)
+        load_x_first(R, 1)
+        load_x_first(Z, 1)
         load_h(1)
         load_xh(0)
         load_xzr(1)
@@ -293,10 +309,14 @@ def tile_gatedgraphconvolution_pb_t_kernel(
                 for_chunk(transpose_h_words, prep_chunk, (block,), "hw_ps")
             if t in (0, 1):
                 transpose_h_words(1, (2 * t, 2 * t + 1), "hw_ps")
-            for_unit(h_minus_cand, t - 3, nc.gpsimd)
+            if t - 3 < N_UNITS - 3:
+                for_unit(h_minus_cand, t - 3, nc.gpsimd)
             for_unit(add_x, t, R, "hr_ps", "pre_r")
+            if t == N_UNITS - 1:
+                sigmoid(t, R, "pre_r", work3, "r")
             for_unit(tanh, t - 2)
-            for_unit(sigmoid, t, R, "pre_r", work3, "r")
+            if t < N_UNITS - 1:
+                for_unit(sigmoid, t, R, "pre_r", work3, "r")
             for_unit(copy_xzr, t + 2)
             if prep_chunk >= 2:
                 for_chunk(group_h_words, prep_chunk, (block,), nc.scalar.copy)
@@ -305,8 +325,10 @@ def tile_gatedgraphconvolution_pb_t_kernel(
             for_unit(add_x, t, Z, "hz_ps", "pre_z")
             for_unit(sigmoid, t, Z, "pre_z", keep, "z")
             for_unit(reset, t - 1)
+            if t - 3 >= N_UNITS - 3:
+                for_unit(h_minus_cand, t - 3, nc.vector)
             for_unit(times_z, t - 3)
-            for_unit(add_and_store, t - 4, engine_for(t - 4, 28))
+            for_unit(add_and_store, t - 4, engine_for(t - 4, N_UNITS - 2))
             if divmod(t + 5, BLOCKS)[1] == 3 and divmod(t + 5, BLOCKS)[0] >= 1:
                 for_chunk(quantise_h, divmod(t + 5, BLOCKS)[0])
             if this_chunk >= 0 and phase == 0:

@@ -84,8 +84,18 @@ def tile_gatedgraphconvolution_pb_t_kernel(
             for b, i in enumerate(blocks):
                 words = chunk_tiles[("h_sb", c)][:, i, :].bitcast(F32)
                 for u in range(2):
-                    nc.tensor.transpose(hw_ps[:, b, u, :], words[:, u : C // 2 : 2], ident_f32[:])
+                    if ("h_sorted", c, i) in chunk_tiles:
+                        nc.tensor.transpose(hw_ps[:, b, u, :], chunk_tiles[("h_sorted", c, i)][:, u, :], ident_f32[:])
+                    else:
+                        nc.tensor.transpose(hw_ps[:, b, u, :], words[:, u : C // 2 : 2], ident_f32[:])
             chunk_tiles[("hw_ps", c, blocks[0])] = hw_ps
+
+        def sort_h_words(c, i):
+            h_sorted = work3.tile([P, 2, P], F32, name="h_sorted")
+            nc.scalar.copy(
+                out=h_sorted[:], in_=chunk_tiles[("h_sb", c)][:, i, :].bitcast(F32).rearrange("p (w u) -> p u w", u=2)
+            )
+            chunk_tiles[("h_sorted", c, i)] = h_sorted
 
         def group_h_words(c, blocks, copy):
             if blocks[0] == 0:
@@ -324,6 +334,8 @@ def tile_gatedgraphconvolution_pb_t_kernel(
                 group_h_words(1, (2 * t, 2 * t + 1), nc.scalar.copy)
             for_unit(add_x, t, Z, "hz_ps", "pre_z")
             for_unit(sigmoid, t, Z, "pre_z", keep, "z")
+            if divmod(t + 7, BLOCKS)[0] >= 2:
+                for_chunk(sort_h_words, divmod(t + 7, BLOCKS)[0], divmod(t + 7, BLOCKS)[1])
             for_unit(reset, t - 1)
             if t - 3 >= N_UNITS - 3:
                 for_unit(h_minus_cand, t - 3, nc.vector)

@@ -25,6 +25,7 @@ N_CHUNKS = NODES // CHUNK
 N_UNITS = N_CHUNKS * COL_TILES
 
 FLOPS = 2 * NODES * C * GATES * C
+EARLY = 4
 
 
 def tile_gatedgraphconvolution_pb_t_kernel(
@@ -124,7 +125,7 @@ def tile_gatedgraphconvolution_pb_t_kernel(
                 xzr_ps = psum.tile([P, 2, CHUNK], BF16, name="zb_ps")
             else:
                 xzr_ps = psum.tile([P, 2, CHUNK], BF16, name="xzr_ps")
-            for g in (Z, R):
+            for g in (R, Z):
                 for i in range(BLOCKS):
                     nc.tensor.transpose(xzr_ps[:, g, i * P : (i + 1) * P], x_block(c, g, j, i), ident_bf16[:])
             unit_tiles[("xzr_ps", n)] = xzr_ps
@@ -258,16 +259,13 @@ def tile_gatedgraphconvolution_pb_t_kernel(
             if 0 <= c < N_CHUNKS:
                 stage(c, *args)
 
-        load_h(0)
-        warm_in = const.tile([P, 1], F32, name="warm_in")
-        nc.vector.memset(warm_in[:], 0.0)
-        warm_out = const.tile([P, 1], F32, name="warm_out")
-        nc.scalar.activation(out=warm_out[:], in_=warm_in[:], func=ACT.Sigmoid)
-        bias_rows = const.tile([P, P], BF16, name="bias_rows")
-        nc.vector.memset(bias_rows[:], 0.0)
-        nc.sync.dma_start(out=bias_rows[0 : GATES * COL_TILES, :], in_=bias_h.rearrange("(r c) -> r c", c=P))
-        load_x_first(R, 0)
-        load_x_first(Z, 0)
+        h_first = loads_h.tile([P, BLOCKS, C], BF16, name="h_sb")
+        chunk_tiles[("h_sb", 0)] = h_first
+        for first in (0, 2):
+            nc.sync.dma_start(
+                out=h_first[:, first : first + 2, :],
+                in_=annotations[0].rearrange("(p i) k -> p i k", i=BLOCKS)[:, first : first + 2, :],
+            )
 
         w_scales = const.tile([P, GATES * C], U8, name="w_scales", align_bytes=64)
         nc.vector.memset(w_scales[:].bitcast(I32), 0)
@@ -278,6 +276,26 @@ def tile_gatedgraphconvolution_pb_t_kernel(
             )
         w_words = const.tile([P, 2 * GATES * C], U8, name="w_words", align_bytes=64)
         nc.sync.dma_start(out=w_words[:].bitcast(I32), in_=recurrent_kernel_words[0].bitcast(I32))
+        load_x_first(R, 0)
+        load_x_first(Z, 0)
+
+        zeros = const.tile([P, CHUNK], BF16, name="zeros")
+        nc.vector.memset(zeros[:], 0.0)
+
+        def idle_matmuls(count):
+            idle_ps = psum.tile([P, CHUNK], F32, name="hz_ps")
+            for k in range(count):
+                nc.tensor.matmul(out=idle_ps[:], lhsT=zeros[:, 0:P], rhs=zeros[:], start=True, stop=True)
+
+        idle_matmuls(EARLY)
+
+        warm_in = const.tile([P, 1], F32, name="warm_in")
+        nc.vector.memset(warm_in[:], 0.0)
+        warm_out = const.tile([P, 1], F32, name="warm_out")
+        nc.scalar.activation(out=warm_out[:], in_=warm_in[:], func=ACT.Sigmoid)
+        bias_rows = const.tile([P, P], BF16, name="bias_rows")
+        nc.vector.memset(bias_rows[:], 0.0)
+        nc.sync.dma_start(out=bias_rows[0 : GATES * COL_TILES, :], in_=bias_h.rearrange("(r c) -> r c", c=P))
         load_x_first(R, 1)
         load_x_first(Z, 1)
         load_h(1)
@@ -286,18 +304,15 @@ def tile_gatedgraphconvolution_pb_t_kernel(
         load_h(2)
         load_xh(1)
 
-        ident_bf16 = const.tile([P, P], BF16, name="ident_bf16")
-        make_identity(nc, ident_bf16[:])
         ident_f32 = const.tile([P, P], F32, name="ident_f32")
         make_identity(nc, ident_f32[:])
-
-        bias_ps = psum.tile([P, 2, CHUNK], BF16, name="xzr_ps")
-        nc.tensor.transpose(bias_ps[:, 0, 0:P], bias_rows[:], ident_bf16[:])
+        ident_bf16 = const.tile([P, P], BF16, name="ident_bf16")
+        make_identity(nc, ident_bf16[:])
         bias_sb = const.tile([P, GATES * COL_TILES], F32, name="bias_sb")
-        nc.vector.tensor_copy(out=bias_sb[:], in_=bias_ps[:, 0, 0 : GATES * COL_TILES])
 
         transpose_h_words(0, (0, 1), "hw_ps")
         transpose_h_words(0, (2, 3), "pc_ps")
+        idle_matmuls(6 - EARLY)
         group_h_words(0, (0, 1), nc.scalar.copy)
         group_h_words(0, (2, 3), nc.vector.tensor_copy)
         quantise_h(0)
@@ -309,6 +324,10 @@ def tile_gatedgraphconvolution_pb_t_kernel(
             prep_chunk, block = divmod(t + 6, BLOCKS)
             this_chunk, phase = divmod(t, BLOCKS)
 
+            if t == 0:
+                bias_ps = psum2.tile([P, 2, CHUNK], BF16, name="hc_ps")
+                nc.tensor.transpose(bias_ps[:, 0, 0:P], bias_rows[:], ident_bf16[:])
+                nc.vector.tensor_copy(out=bias_sb[:], in_=bias_ps[:, 0, 0 : GATES * COL_TILES])
             for_unit(multiply, t, R, "hr_ps")
             for_unit(multiply, t, Z, "hz_ps")
             for_unit(multiply, t - 1, CAND, "hc_ps")

from contextlib import ExitStack

import concourse.mybir as mybir
from concourse.masks import make_identity

F32 = mybir.dt.float32
BF16 = mybir.dt.bfloat16
I32 = mybir.dt.int32
U8 = mybir.dt.uint8
U32 = mybir.dt.uint32
FP8X4 = mybir.dt.float8_e4m3fn_x4
FP4X4 = mybir.dt.float4_e2m1fn_x4
ALU = mybir.AluOpType
ACT = mybir.ActivationFunctionType

P = 128
C = 512
GATES = 3
Z, R, CAND = 0, 1, 2
NODES = 4096
CHUNK = 512
BLOCKS = CHUNK // P
COL_TILES = C // P
N_CHUNKS = NODES // CHUNK
N_UNITS = N_CHUNKS * COL_TILES

FLOPS = 2 * NODES * C * GATES * C
EARLY = 4


def tile_gatedgraphconvolution_pb_t_kernel(
    tc, x_proj, annotations, recurrent_kernel_words, recurrent_kernel_scales, bias_h, out
):
    nc = tc.nc
    with ExitStack() as stack:
        const = stack.enter_context(tc.tile_pool(name="const", bufs=1))
        loads_xzr = stack.enter_context(tc.tile_pool(name="loads_xzr", bufs=3))
        loads_xh = stack.enter_context(tc.tile_pool(name="loads_xh", bufs=4))
        loads_h = stack.enter_context(tc.tile_pool(name="loads_h", bufs=6))
        quant = stack.enter_context(tc.tile_pool(name="quant", bufs=2))
        work2 = stack.enter_context(tc.tile_pool(name="work2", bufs=2))
        work3 = stack.enter_context(tc.tile_pool(name="work3", bufs=3))
        outs = stack.enter_context(tc.tile_pool(name="outs", bufs=3))
        work6 = stack.enter_context(tc.tile_pool(name="work6", bufs=6))
        keep = stack.enter_context(tc.tile_pool(name="keep", bufs=10))
        psum = stack.enter_context(tc.psum_pool(name="psum", bufs=1))
        psum2 = stack.enter_context(tc.psum_pool(name="psum2", bufs=2))
        stack.enter_context(tc.manual_schedule())

        chunk_tiles = {}
        unit_tiles = {}

        def load_h(c):
            h_sb = loads_h.tile([P, BLOCKS, C], BF16, name="h_sb")
            nc.sync.dma_start(out=h_sb[:], in_=annotations[c].rearrange("(p i) k -> p i k", i=BLOCKS))
            chunk_tiles[("h_sb", c)] = h_sb

        def load_xzr(c):
            xzr_in = loads_xzr.tile([P, BLOCKS, 2 * C], BF16, name="xzr_in")
            rows = x_proj[c * CHUNK : (c + 1) * CHUNK, 0 : 2 * C]
            nc.sync.dma_start(out=xzr_in[:], in_=rows.rearrange("(p i) g -> p i g", i=BLOCKS))
            chunk_tiles[("xzr_in", c)] = xzr_in

        def load_x_first(g, half):
            part = const.tile([P, BLOCKS, 2 * P], BF16, name="x_first_%d_%d" % (g, half))
            first = g * C + half * 2 * P
            rows = x_proj[0:CHUNK, first : first + 2 * P]
            nc.sync.dma_start(out=part[:], in_=rows.rearrange("(p i) g -> p i g", i=BLOCKS))
            chunk_tiles[("x_first", g, half)] = part

        def x_block(c, g, j, i):
            if c == 0:
                return chunk_tiles[("x_first", g, j // 2)][:, i, (j % 2) * P : (j % 2 + 1) * P]
            first = g * C + j * P
            return chunk_tiles[("xzr_in", c)][:, i, first : first + P]

        def load_xh(c):
            xh_in = loads_xh.tile([P, BLOCKS, C], BF16, name="xh_in")
            rows = x_proj[c * CHUNK : (c + 1) * CHUNK, CAND * C : (CAND + 1) * C]
            nc.sync.dma_start(out=xh_in[:], in_=rows.rearrange("(p i) g -> p i g", i=BLOCKS))
            chunk_tiles[("xh_in", c)] = xh_in

        def transpose_h_words(c, blocks, name):
            hw_ps = psum.tile([P, len(blocks), 2, P], F32, name=name)
            for b, i in enumerate(blocks):
                words = chunk_tiles[("h_sb", c)][:, i, :].bitcast(F32)
                for u in range(2):
                    if ("h_sorted", c, i) in chunk_tiles:
                        nc.tensor.transpose(hw_ps[:, b, u, :], chunk_tiles[("h_sorted", c, i)][:, u, :], ident_f32[:])
                    else:
                        nc.tensor.transpose(hw_ps[:, b, u, :], words[:, u : C // 2 : 2], ident_f32[:])
            chunk_tiles[("hw_ps", c, blocks[0])] = hw_ps

        def sort_h_words(c, i):
            h_sorted = work3.tile([P, 2, P], F32, name="h_sorted")
            nc.scalar.copy(
                out=h_sorted[:], in_=chunk_tiles[("h_sb", c)][:, i, :].bitcast(F32).rearrange("p (w u) -> p u w", u=2)
            )
            chunk_tiles[("h_sorted", c, i)] = h_sorted

        def group_h_words(c, blocks, copy):
            if blocks[0] == 0:
                grouped_new = quant.tile([P, CHUNK * 4], BF16, name="grouped", align_bytes=64)
                chunk_tiles[("grouped", c)] = grouped_new
            grouped = chunk_tiles[("grouped", c)]
            as_words = grouped[:].bitcast(F32).rearrange("p (i r u) -> p i r u", i=BLOCKS, u=2)
            hw_ps = chunk_tiles[("hw_ps", c, blocks[0])]
            copy(
                out=as_words[:, blocks[0] : blocks[0] + len(blocks)],
                in_=hw_ps[:].rearrange("p b u r -> p b r u"),
            )

        def quantise_h(c):
            codes = quant.tile([P, CHUNK], U32, name="codes", align_bytes=64)
            scales = quant.tile([P, CHUNK], U8, name="scales", align_bytes=64)
            nc.vector.quantize_mx(
                out=codes[:].bitcast(FP8X4), scales=scales[:], in_=chunk_tiles[("grouped", c)][:]
            )
            chunk_tiles[("codes", c)] = codes
            chunk_tiles[("scales", c)] = scales

        def transpose_x(n):
            c, j = divmod(n, COL_TILES)
            if n == 1:
                xzr_ps = psum.tile([P, 2, CHUNK], BF16, name="zb_ps")
            else:
                xzr_ps = psum.tile([P, 2, CHUNK], BF16, name="xzr_ps")
            for g in (R, Z):
                for i in range(BLOCKS):
                    nc.tensor.transpose(xzr_ps[:, g, i * P : (i + 1) * P], x_block(c, g, j, i), ident_bf16[:])
            unit_tiles[("xzr_ps", n)] = xzr_ps

        def copy_xzr(n):
            xzr_sb = work3.tile([P, 2, CHUNK], BF16, name="xzr_sb")
            nc.scalar.copy(out=xzr_sb[:], in_=unit_tiles[("xzr_ps", n)][:])
            unit_tiles[("xzr_sb", n)] = xzr_sb

        def multiply(n, g, name):
            c, j = divmod(n, COL_TILES)
            first = g * C + j * P
            acc = (psum2 if g == CAND else psum).tile([P, CHUNK], F32, name=name)
            nc.tensor.matmul_mx(
                out=acc[:],
                lhsT=w_words[:, 2 * first : 2 * (first + P)].bitcast(FP4X4),
                lhsT_scale=w_scales[:, first : first + P],
                rhs=chunk_tiles[("codes", c)][:].bitcast(FP8X4),
                rhs_scale=chunk_tiles[("scales", c)][:],
                start=True,
                stop=True,
            )
            unit_tiles[(name, n)] = acc

        def bias_of(g, n):
            column = g * COL_TILES + n % COL_TILES
            return bias_sb[:, column : column + 1]

        def add_x(n, g, acc_name, name):
            pre = work2.tile([P, CHUNK], F32, name=name)
            nc.vector.tensor_tensor(
                out=pre[:], in0=unit_tiles[(acc_name, n)][:], in1=unit_tiles[("xzr_sb", n)][:, g, :], op=ALU.add
            )
            unit_tiles[(name, n)] = pre

        def sigmoid(n, g, pre_name, pool, name):
            gate = pool.tile([P, CHUNK], F32, name=name)
            nc.scalar.activation(
                out=gate[:], in_=unit_tiles[(pre_name, n)][:], func=ACT.Sigmoid, bias=bias_of(g, n), scale=1.0
            )
            unit_tiles[(name, n)] = gate

        def reset(n):
            rh = keep.tile([P, CHUNK], F32, name="rh")
            nc.vector.scalar_tensor_tensor(
                out=rh[:],
                in0=unit_tiles[("hc_ps", n)][:],
                scalar=bias_of(CAND, n),
                in1=unit_tiles[("r", n)][:],
                op0=ALU.add,
                op1=ALU.mult,
            )
            unit_tiles[("rh", n)] = rh

        def cols_of(n):
            j = n % COL_TILES
            return slice(j * P, (j + 1) * P)

        def candidate_input(n):
            c = n // COL_TILES
            pc_ps = psum.tile([P, BLOCKS, P], F32, name={N_UNITS - 2: "hz_ps", N_UNITS - 1: "hr_ps"}.get(n, "pc_ps"))
            nc.tensor.matmul(
                out=pc_ps[:],
                lhsT=ident_bf16[:],
                rhs=chunk_tiles[("xh_in", c)][:, :, cols_of(n)],
                start=True,
                stop=False,
            )
            for i in range(BLOCKS):
                nc.tensor.matmul(
                    out=pc_ps[:, i, :],
                    lhsT=unit_tiles[("rh", n)][:, i * P : (i + 1) * P],
                    rhs=ident_f32[:],
                    is_transpose=True,
                    start=False,
                    stop=(i == BLOCKS - 1),
                )
            unit_tiles[("pc_ps", n)] = pc_ps

        def tanh(n):
            cand = work6.tile([P, BLOCKS, P], F32, name="cand")
            nc.scalar.activation(out=cand[:], in_=unit_tiles[("pc_ps", n)][:], func=ACT.Tanh)
            unit_tiles[("cand", n)] = cand

        def transpose_z(n):
            zb_ps = psum.tile([P, BLOCKS, P], F32, name={N_UNITS - 2: "xzr_ps", N_UNITS - 1: "hw_ps"}.get(n, "zb_ps"))
            for i in range(BLOCKS):
                nc.tensor.transpose(
                    zb_ps[:, i, :], unit_tiles[("z", n)][:, i * P : (i + 1) * P], ident_f32[:]
                )
            unit_tiles[("zb_ps", n)] = zb_ps

        def h_minus_cand(n, eng):
            c = n // COL_TILES
            diff = work3.tile([P, BLOCKS, P], F32, name="diff")
            eng.tensor_tensor(
                out=diff[:],
                in0=chunk_tiles[("h_sb", c)][:, :, cols_of(n)],
                in1=unit_tiles[("cand", n)][:],
                op=ALU.subtract,
            )
            unit_tiles[("diff", n)] = diff

        def times_z(n):
            zd = work3.tile([P, BLOCKS, P], F32, name="zd")
            nc.vector.tensor_tensor(
                out=zd[:], in0=unit_tiles[("zb_ps", n)][:], in1=unit_tiles[("diff", n)][:], op=ALU.mult
            )
            unit_tiles[("zd", n)] = zd

        def add_and_store(n, eng):
            c, j = divmod(n, COL_TILES)
            if j == 0:
                out_new = outs.tile([P, BLOCKS, C], F32, name="out_sb")
                chunk_tiles[("out_sb", c)] = out_new
            out_sb = chunk_tiles[("out_sb", c)]
            eng.tensor_tensor(
                out=out_sb[:, :, cols_of(n)], in0=unit_tiles[("zd", n)][:], in1=unit_tiles[("cand", n)][:], op=ALU.add
            )
            rows = out[c].rearrange("(p i) k -> p i k", i=BLOCKS)
            if c == N_CHUNKS - 1:
                nc.sync.dma_start(out=rows[:, :, cols_of(n)], in_=out_sb[:, :, cols_of(n)])
            elif j == COL_TILES - 1:
                nc.sync.dma_start(out=rows, in_=out_sb[:])

        def for_unit(stage, n, *args):
            if 0 <= n < N_UNITS:
                stage(n, *args)

        def for_chunk(stage, c, *args):
            if 0 <= c < N_CHUNKS:
                stage(c, *args)

        h_first = loads_h.tile([P, BLOCKS, C], BF16, name="h_sb")
        chunk_tiles[("h_sb", 0)] = h_first
        for first in (0, 2):
            nc.sync.dma_start(
                out=h_first[:, first : first + 2, :],
                in_=annotations[0].rearrange("(p i) k -> p i k", i=BLOCKS)[:, first : first + 2, :],
            )

        w_scales = const.tile([P, GATES * C], U8, name="w_scales", align_bytes=64)
        nc.vector.memset(w_scales[:].bitcast(I32), 0)
        for quadrant in range(4):
            nc.sync.dma_start(
                out=w_scales[32 * quadrant : 32 * quadrant + 4, :].bitcast(I32),
                in_=recurrent_kernel_scales[0, 4 * quadrant : 4 * quadrant + 4, :].bitcast(I32),
            )
        w_words = const.tile([P, 2 * GATES * C], U8, name="w_words", align_bytes=64)
        nc.sync.dma_start(out=w_words[:].bitcast(I32), in_=recurrent_kernel_words[0].bitcast(I32))
        load_x_first(R, 0)
        load_x_first(Z, 0)

        zeros = const.tile([P, CHUNK], BF16, name="zeros")
        nc.vector.memset(zeros[:], 0.0)

        def idle_matmuls(count):
            idle_ps = psum.tile([P, CHUNK], F32, name="hz_ps")
            for k in range(count):
                nc.tensor.matmul(out=idle_ps[:], lhsT=zeros[:, 0:P], rhs=zeros[:], start=True, stop=True)

        idle_matmuls(EARLY)

        warm_in = const.tile([P, 1], F32, name="warm_in")
        nc.vector.memset(warm_in[:], 0.0)
        warm_out = const.tile([P, 1], F32, name="warm_out")
        nc.scalar.activation(out=warm_out[:], in_=warm_in[:], func=ACT.Sigmoid)
        bias_rows = const.tile([P, P], BF16, name="bias_rows")
        nc.vector.memset(bias_rows[:], 0.0)
        nc.sync.dma_start(out=bias_rows[0 : GATES * COL_TILES, :], in_=bias_h.rearrange("(r c) -> r c", c=P))
        load_x_first(R, 1)
        load_x_first(Z, 1)
        load_h(1)
        load_xh(0)
        load_xzr(1)
        load_h(2)
        load_xh(1)

        ident_f32 = const.tile([P, P], F32, name="ident_f32")
        make_identity(nc, ident_f32[:])
        ident_bf16 = const.tile([P, P], BF16, name="ident_bf16")
        make_identity(nc, ident_bf16[:])
        bias_sb = const.tile([P, GATES * COL_TILES], F32, name="bias_sb")

        transpose_h_words(0, (0, 1), "hw_ps")
        transpose_h_words(0, (2, 3), "pc_ps")
        idle_matmuls(6 - EARLY)
        group_h_words(0, (0, 1), nc.scalar.copy)
        group_h_words(0, (2, 3), nc.vector.tensor_copy)
        quantise_h(0)

        def engine_for(m, first):
            return nc.vector if m >= first else nc.gpsimd

        for t in range(-3, N_UNITS + 5):
            prep_chunk, block = divmod(t + 6, BLOCKS)
            this_chunk, phase = divmod(t, BLOCKS)

            if t == 0:
                bias_ps = psum2.tile([P, 2, CHUNK], BF16, name="hc_ps")
                nc.tensor.transpose(bias_ps[:, 0, 0:P], bias_rows[:], ident_bf16[:])
                nc.vector.tensor_copy(out=bias_sb[:], in_=bias_ps[:, 0, 0 : GATES * COL_TILES])
            for_unit(multiply, t, R, "hr_ps")
            for_unit(multiply, t, Z, "hz_ps")
            for_unit(multiply, t - 1, CAND, "hc_ps")
            for_unit(candidate_input, t - 2)
            for_unit(transpose_z, t - 3)
            for_unit(transpose_x, t + 2)
            if prep_chunk >= 2:
                for_chunk(transpose_h_words, prep_chunk, (block,), "hw_ps")
            if t in (0, 1):
                transpose_h_words(1, (2 * t, 2 * t + 1), "hw_ps")
            if t - 3 < N_UNITS - 3:
                for_unit(h_minus_cand, t - 3, nc.gpsimd)
            for_unit(add_x, t, R, "hr_ps", "pre_r")
            if t == N_UNITS - 1:
                sigmoid(t, R, "pre_r", work3, "r")
            for_unit(tanh, t - 2)
            if t < N_UNITS - 1:
                for_unit(sigmoid, t, R, "pre_r", work3, "r")
            for_unit(copy_xzr, t + 2)
            if prep_chunk >= 2:
                for_chunk(group_h_words, prep_chunk, (block,), nc.scalar.copy)
            if t in (0, 1):
                group_h_words(1, (2 * t, 2 * t + 1), nc.scalar.copy)
            for_unit(add_x, t, Z, "hz_ps", "pre_z")
            for_unit(sigmoid, t, Z, "pre_z", keep, "z")
            if divmod(t + 7, BLOCKS)[0] >= 2:
                for_chunk(sort_h_words, divmod(t + 7, BLOCKS)[0], divmod(t + 7, BLOCKS)[1])
            for_unit(reset, t - 1)
            if t - 3 >= N_UNITS - 3:
                for_unit(h_minus_cand, t - 3, nc.vector)
            for_unit(times_z, t - 3)
            for_unit(add_and_store, t - 4, engine_for(t - 4, N_UNITS - 2))
            if divmod(t + 5, BLOCKS)[1] == 3 and divmod(t + 5, BLOCKS)[0] >= 1:
                for_chunk(quantise_h, divmod(t + 5, BLOCKS)[0])
            if this_chunk >= 0 and phase == 0:
                for_chunk(load_h, this_chunk + 3)
            if this_chunk >= 0 and phase == 1:
                for_chunk(load_xzr, this_chunk + 2)
            if this_chunk >= 0 and phase == 2:
                for_chunk(load_xh, this_chunk + 2)
